import numpy as np
import ml_dtypes


def mxq(x, axis, fmt="e4m3"):
    dtype, down = {"e4m3": (ml_dtypes.float8_e4m3fn, 7), "e5m2": (ml_dtypes.float8_e5m2, 14)}[fmt]
    v = np.moveaxis(np.asarray(x, np.float32).astype(ml_dtypes.bfloat16).astype(np.float64), axis, -1)
    blocks = v.reshape(v.shape[:-1] + (-1, 32))
    amax = np.abs(blocks).max(-1, keepdims=True)
    byte = np.maximum(np.where(amax > 0, np.frexp(amax)[1] - 1 + 127, 0) - down, 1)
    scale = np.exp2(byte - 127.0)
    codes = (blocks / scale).astype(np.float32).astype(dtype).astype(np.float64)
    return np.moveaxis((codes * scale).reshape(v.shape), -1, axis)


WIDE = False


def mx_kscale(k):
    if not WIDE:
        return np.ones(k)
    levels = np.array([10, -10, 5, -5, 0])
    a = np.random.permutation(np.resize(levels, k // 512 * 4)).reshape(k // 512, 4)
    idx = np.arange(k)
    return np.exp2(a[idx // 512, idx % 128 // 32])


BF16 = ml_dtypes.bfloat16


def bf(x):
    return np.asarray(x, np.float32).astype(BF16)


def f64(x):
    return np.asarray(x).astype(np.float64)


B, C, H, W, O, K = 2, 512, 8, 16, 256, 3
DIRS = [(0, 1), (1, 1), (1, 0), (1, -1), (0, -1), (-1, -1), (-1, 0), (-1, 1)]
DILATION = 1
CENTER = K // 2
PAD = CENTER * DILATION


def setup_inputs():
    s = mx_kscale(C)
    bound = np.sqrt(6.0 / (C * K))
    return {"x": bf(np.random.standard_normal((B, C, H, W)) * s[None, :, None, None]),
            "weight": bf(np.random.uniform(-bound, bound, (O, C, K)) / s[None, :, None])}


def reference(x, weight):
    xq = mxq(f64(x).reshape(B, C, H * W), 1, "e4m3")
    wq = mxq(f64(weight).transpose(2, 0, 1).reshape(K * O, C), 1, "e4m3")
    y = (wq @ xq).reshape(B, K, O, H, W)
    yp = np.pad(y, ((0, 0), (0, 0), (0, 0), (PAD, PAD), (PAD, PAD)))
    outs = []
    for dy, dx in DIRS:
        acc = np.zeros((B, O, H, W))
        for k in range(K):
            r0 = PAD + (k - CENTER) * DILATION * dy
            c0 = PAD + (k - CENTER) * DILATION * dx
            acc = acc + yp[:, k, :, r0: r0 + H, c0: c0 + W]
        outs.append(acc)
    return np.stack(outs, axis=2)

@@ -1,0 +1,135 @@
+from contextlib import ExitStack
+
+import concourse.mybir as mybir
+from concourse.masks import make_identity
+
+BF16 = mybir.dt.bfloat16
+F32 = mybir.dt.float32
+U32 = mybir.dt.uint32
+U8 = mybir.dt.uint8
+FP8X4 = mybir.dt.float8_e4m3fn_x4
+
+B, C, H, W, O, TAPS = 2, 512, 8, 16, 256, 3
+STEPS = ((0, 1), (1, 1), (1, 0), (1, -1), (0, -1), (-1, -1), (-1, 0), (-1, 1))
+N_STEPS = len(STEPS)
+
+P = 128
+PACK = 4
+PIXELS = H * W
+O_TILES = O // P
+STEPS_PER_BANK = 4
+N_COPIES = N_STEPS + STEPS_PER_BANK
+
+FLOPS = 2 * B * H * W * C * O * TAPS
+
+
+def tile_r8convf_pa_s_kernel(tc, x, weight, out):
+    nc = tc.nc
+    with ExitStack() as ctx:
+        ctx.enter_context(tc.manual_schedule())
+        keep = ctx.enter_context(tc.tile_pool(name="keep", bufs=1))
+        stage = ctx.enter_context(tc.tile_pool(name="stage", bufs=4))
+        psum = ctx.enter_context(tc.psum_pool(name="psum", bufs=8))
+
+        identity = keep.tile([P, P], BF16)
+        x_raw = keep.tile([P, B, PACK, H, W], BF16)
+        w_raw = keep.tile([P, O_TILES, C, TAPS], BF16)
+        x_moved = keep.tile([P, 3, B, H + 2, W, PACK], BF16, align_bytes=64)
+        x_codes = keep.tile([P, B, N_COPIES * PIXELS], U32, align_bytes=64)
+        x_scales = keep.tile([P, B, N_COPIES * PIXELS], U8, align_bytes=64)
+        w_grouped = keep.tile([P, O_TILES, TAPS, P, PACK], BF16, align_bytes=64)
+        w_codes = keep.tile([P, O_TILES, TAPS, P], U32, align_bytes=64)
+        w_scales = keep.tile([P, O_TILES, TAPS, P], U8, align_bytes=64)
+
+        def load_x(b):
+            nc.scalar.dma_start(
+                out=x_raw[:, b].rearrange("p t h w -> p t (h w)"),
+                in_=x[b].rearrange("(t p) h w -> p t (h w)", p=P),
+            )
+
+        def load_weight(ot):
+            nc.sync.dma_start(
+                out=w_raw[:, ot].rearrange("p c k -> p (c k)"),
+                in_=weight[ot * P : (ot + 1) * P].rearrange("o c k -> o (c k)"),
+            )
+
+        def move_x(b):
+            for dx in (-1, 0, 1):
+                first, last = max(0, -dx), W - max(0, dx)
+                nc.vector.tensor_copy(
+                    out=x_moved[:, dx + 1, b, 1 : 1 + H, first:last, :],
+                    in_=x_raw[:, b, :, :, first + dx : last + dx].rearrange("p t h w -> p h w t"),
+                )
+
+        def quantise_copy(b, copy, dy, dx):
+            columns = slice(copy * PIXELS, (copy + 1) * PIXELS)
+            nc.vector.quantize_mx(
+                out=x_codes[:, b, columns].bitcast(FP8X4),
+                scales=x_scales[:, b, columns],
+                in_=x_moved[:, dx + 1, b, 1 + dy : 1 + dy + H].rearrange("p h w t -> p (h w t)"),
+            )
+
+        def quantise_x(b):
+            for d, (dy, dx) in enumerate(STEPS):
+                quantise_copy(b, d, dy, dx)
+            for copy in range(N_STEPS, N_COPIES):
+                quantise_copy(b, copy, 0, 0)
+
+        def transpose_weight(ot):
+            for k in range(TAPS):
+                w_t = psum.tile([P, PACK, P], BF16, tag="bank", name="w_t")
+                for t in range(PACK):
+                    nc.tensor.transpose(w_t[:, t, :], w_raw[:, ot, t * P : (t + 1) * P, k], identity[:])
+                nc.scalar.copy(out=w_grouped[:, ot, k], in_=w_t[:].rearrange("p t o -> p o t"))
+
+        def quantise_weight(ot):
+            for k in range(TAPS):
+                nc.vector.quantize_mx(
+                    out=w_codes[:, ot, k].bitcast(FP8X4),
+                    scales=w_scales[:, ot, k],
+                    in_=w_grouped[:, ot, k].rearrange("p o t -> p (o t)"),
+                )
+
+        def convolve(ot, b):
+            for d0 in range(0, N_STEPS, STEPS_PER_BANK):
+                first_copy = {0: (d0 + N_STEPS // 2) % N_STEPS, 1: N_STEPS, 2: d0}
+                acc = psum.tile([P, STEPS_PER_BANK * PIXELS], F32, tag="bank", name="acc")
+                for k in range(TAPS):
+                    columns = slice(first_copy[k] * PIXELS, (first_copy[k] + STEPS_PER_BANK) * PIXELS)
+                    nc.tensor.matmul_mx(
+                        out=acc[:],
+                        lhsT=w_codes[:, ot, k].bitcast(FP8X4),
+                        lhsT_scale=w_scales[:, ot, k],
+                        rhs=x_codes[:, b, columns].bitcast(FP8X4),
+                        rhs_scale=x_scales[:, b, columns],
+                        start=(k == 0),
+                        stop=(k == TAPS - 1),
+                    )
+                result = stage.tile([P, STEPS_PER_BANK * PIXELS], F32)
+                nc.scalar.copy(out=result[:], in_=acc[:])
+                nc.sync.dma_start(
+                    out=out[b, ot * P : (ot + 1) * P, d0 : d0 + STEPS_PER_BANK].rearrange(
+                        "o d h w -> o (d h w)"
+                    ),
+                    in_=result[:],
+                )
+
+        for b in range(B):
+            load_x(b)
+        for ot in range(O_TILES):
+            load_weight(ot)
+        make_identity(nc, identity[:])
+        nc.vector.memset(x_moved[:], 0.0)
+
+        move_x(0)
+        transpose_weight(0)
+        quantise_x(0)
+        transpose_weight(1)
+        quantise_weight(0)
+        move_x(1)
+        quantise_weight(1)
+        convolve(0, 0)
+        convolve(1, 0)
+        quantise_x(1)
+        convolve(0, 1)
+        convolve(1, 1)

@@ -5,6 +5,7 @@ from concourse.masks import make_identity
 
 BF16 = mybir.dt.bfloat16
 F32 = mybir.dt.float32
+I32 = mybir.dt.int32
 U32 = mybir.dt.uint32
 U8 = mybir.dt.uint8
 FP8X4 = mybir.dt.float8_e4m3fn_x4
@@ -12,15 +13,17 @@ FP8X4 = mybir.dt.float8_e4m3fn_x4
 B, C, H, W, O, TAPS = 2, 512, 8, 16, 256, 3
 STEPS = ((0, 1), (1, 1), (1, 0), (1, -1), (0, -1), (-1, -1), (-1, 0), (-1, 1))
 N_STEPS = len(STEPS)
+HALF_TURN = N_STEPS // 2
 
 P = 128
 PACK = 4
-PIXELS = H * W
+PIXELS = B * H * W
 O_TILES = O // P
-STEPS_PER_BANK = 4
-N_COPIES = N_STEPS + STEPS_PER_BANK
+UNMOVED = N_STEPS
+N_COPIES = N_STEPS + 1
+STEPS_PER_STORE = 2
 
-FLOPS = 2 * B * H * W * C * O * TAPS
+FLOPS = 2 * PIXELS * C * O * TAPS
 
 
 def tile_r8convf_pa_s_kernel(tc, x, weight, out):
@@ -34,9 +37,9 @@ def tile_r8convf_pa_s_kernel(tc, x, weight, out):
         identity = keep.tile([P, P], BF16)
         x_raw = keep.tile([P, B, PACK, H, W], BF16)
         w_raw = keep.tile([P, O_TILES, C, TAPS], BF16)
-        x_moved = keep.tile([P, 3, B, H + 2, W, PACK], BF16, align_bytes=64)
-        x_codes = keep.tile([P, B, N_COPIES * PIXELS], U32, align_bytes=64)
-        x_scales = keep.tile([P, B, N_COPIES * PIXELS], U8, align_bytes=64)
+        x_moved = keep.tile([P, 3, H + 2, B, W, PACK], BF16, align_bytes=64)
+        x_codes = keep.tile([P, N_COPIES, PIXELS], U32, align_bytes=64)
+        x_scales = keep.tile([P, N_COPIES, PIXELS], U8, align_bytes=64)
         w_grouped = keep.tile([P, O_TILES, TAPS, P, PACK], BF16, align_bytes=64)
         w_codes = keep.tile([P, O_TILES, TAPS, P], U32, align_bytes=64)
         w_scales = keep.tile([P, O_TILES, TAPS, P], U8, align_bytes=64)
@@ -53,27 +56,23 @@ def tile_r8convf_pa_s_kernel(tc, x, weight, out):
                 in_=weight[ot * P : (ot + 1) * P].rearrange("o c k -> o (c k)"),
             )
 
-        def move_x(b):
-            for dx in (-1, 0, 1):
-                first, last = max(0, -dx), W - max(0, dx)
-                nc.vector.tensor_copy(
-                    out=x_moved[:, dx + 1, b, 1 : 1 + H, first:last, :],
-                    in_=x_raw[:, b, :, :, first + dx : last + dx].rearrange("p t h w -> p h w t"),
-                )
-
-        def quantise_copy(b, copy, dy, dx):
-            columns = slice(copy * PIXELS, (copy + 1) * PIXELS)
-            nc.vector.quantize_mx(
-                out=x_codes[:, b, columns].bitcast(FP8X4),
-                scales=x_scales[:, b, columns],
-                in_=x_moved[:, dx + 1, b, 1 + dy : 1 + dy + H].rearrange("p h w t -> p (h w t)"),
+        def move_x(dx):
+            first, last = max(0, -dx), W - max(0, dx)
+            nc.vector.tensor_copy(
+                out=x_moved[:, dx + 1, 1 : 1 + H, :, first:last, :],
+                in_=x_raw[:, :, :, :, first + dx : last + dx].rearrange("p b t h w -> p h b w t"),
             )
 
-        def quantise_x(b):
-            for d, (dy, dx) in enumerate(STEPS):
-                quantise_copy(b, d, dy, dx)
-            for copy in range(N_STEPS, N_COPIES):
-                quantise_copy(b, copy, 0, 0)
+        def quantise_copy(copy, dy, dx):
+            nc.vector.quantize_mx(
+                out=x_codes[:, copy].bitcast(FP8X4),
+                scales=x_scales[:, copy],
+                in_=x_moved[:, dx + 1, 1 + dy : 1 + dy + H].rearrange("p h b w t -> p (h b w t)"),
+            )
+
+        def quantise_opposite_copies(d):
+            for copy in (d + HALF_TURN, d):
+                quantise_copy(copy, STEPS[copy][0], STEPS[copy][1])
 
         def transpose_weight(ot):
             for k in range(TAPS):
@@ -90,28 +89,31 @@ def tile_r8convf_pa_s_kernel(tc, x, weight, out):
                     in_=w_grouped[:, ot, k].rearrange("p o t -> p (o t)"),
                 )
 
-        def convolve(ot, b):
-            for d0 in range(0, N_STEPS, STEPS_PER_BANK):
-                first_copy = {0: (d0 + N_STEPS // 2) % N_STEPS, 1: N_STEPS, 2: d0}
-                acc = psum.tile([P, STEPS_PER_BANK * PIXELS], F32, tag="bank", name="acc")
-                for k in range(TAPS):
-                    columns = slice(first_copy[k] * PIXELS, (first_copy[k] + STEPS_PER_BANK) * PIXELS)
-                    nc.tensor.matmul_mx(
-                        out=acc[:],
-                        lhsT=w_codes[:, ot, k].bitcast(FP8X4),
-                        lhsT_scale=w_scales[:, ot, k],
-                        rhs=x_codes[:, b, columns].bitcast(FP8X4),
-                        rhs_scale=x_scales[:, b, columns],
-                        start=(k == 0),
-                        stop=(k == TAPS - 1),
+        def convolve(ot):
+            for d0 in range(0, N_STEPS, STEPS_PER_STORE):
+                result = stage.tile([P, B, STEPS_PER_STORE, H, W], F32)
+                for i in range(STEPS_PER_STORE):
+                    d = d0 + i
+                    copy_of_tap = ((d + HALF_TURN) % N_STEPS, UNMOVED, d)
+                    acc = psum.tile([P, PIXELS], F32, tag="bank", name="acc")
+                    for k in range(TAPS):
+                        nc.tensor.matmul_mx(
+                            out=acc[:],
+                            lhsT=w_codes[:, ot, k].bitcast(FP8X4),
+                            lhsT_scale=w_scales[:, ot, k],
+                            rhs=x_codes[:, copy_of_tap[k]].bitcast(FP8X4),
+                            rhs_scale=x_scales[:, copy_of_tap[k]],
+                            start=(k == 0),
+                            stop=(k == TAPS - 1),
+                        )
+                    nc.scalar.copy(
+                        out=result[:, :, i], in_=acc[:].rearrange("p (h b w) -> p b h w", h=H, b=B)
                     )
-                result = stage.tile([P, STEPS_PER_BANK * PIXELS], F32)
-                nc.scalar.copy(out=result[:], in_=acc[:])
                 nc.sync.dma_start(
-                    out=out[b, ot * P : (ot + 1) * P, d0 : d0 + STEPS_PER_BANK].rearrange(
-                        "o d h w -> o (d h w)"
+                    out=out[:, ot * P : (ot + 1) * P, d0 : d0 + STEPS_PER_STORE].rearrange(
+                        "b o d h w -> o b (d h w)"
                     ),
-                    in_=result[:],
+                    in_=result[:].rearrange("p b d h w -> p b (d h w)"),
                 )
 
         for b in range(B):
@@ -119,17 +121,18 @@ def tile_r8convf_pa_s_kernel(tc, x, weight, out):
         for ot in range(O_TILES):
             load_weight(ot)
         make_identity(nc, identity[:])
-        nc.vector.memset(x_moved[:], 0.0)
+        nc.vector.memset(x_moved[:].rearrange("p a h b w t -> p (a h b w t)").bitcast(I32), 0)
 
-        move_x(0)
+        for dx in (-1, 0, 1):
+            move_x(dx)
         transpose_weight(0)
-        quantise_x(0)
+        quantise_copy(UNMOVED, 0, 0)
+        quantise_opposite_copies(0)
+        quantise_opposite_copies(1)
         transpose_weight(1)
         quantise_weight(0)
-        move_x(1)
+        quantise_opposite_copies(2)
+        quantise_opposite_copies(3)
         quantise_weight(1)
-        convolve(0, 0)
-        convolve(1, 0)
-        quantise_x(1)
-        convolve(0, 1)
-        convolve(1, 1)
+        convolve(0)
+        convolve(1)

@@ -13,17 +13,15 @@ FP8X4 = mybir.dt.float8_e4m3fn_x4
 B, C, H, W, O, TAPS = 2, 512, 8, 16, 256, 3
 STEPS = ((0, 1), (1, 1), (1, 0), (1, -1), (0, -1), (-1, -1), (-1, 0), (-1, 1))
 N_STEPS = len(STEPS)
-HALF_TURN = N_STEPS // 2
 
 P = 128
 PACK = 4
-PIXELS = B * H * W
+PIXELS = H * W
 O_TILES = O // P
-UNMOVED = N_STEPS
-N_COPIES = N_STEPS + 1
-STEPS_PER_STORE = 2
+STEPS_PER_BANK = 4
+N_COPIES = N_STEPS + STEPS_PER_BANK
 
-FLOPS = 2 * PIXELS * C * O * TAPS
+FLOPS = 2 * B * H * W * C * O * TAPS
 
 
 def tile_r8convf_pa_s_kernel(tc, x, weight, out):
@@ -37,15 +35,15 @@ def tile_r8convf_pa_s_kernel(tc, x, weight, out):
         identity = keep.tile([P, P], BF16)
         x_raw = keep.tile([P, B, PACK, H, W], BF16)
         w_raw = keep.tile([P, O_TILES, C, TAPS], BF16)
-        x_moved = keep.tile([P, 3, H + 2, B, W, PACK], BF16, align_bytes=64)
-        x_codes = keep.tile([P, N_COPIES, PIXELS], U32, align_bytes=64)
-        x_scales = keep.tile([P, N_COPIES, PIXELS], U8, align_bytes=64)
+        x_moved = keep.tile([P, B, 3, H + 2, W, PACK], BF16, align_bytes=64)
+        x_codes = keep.tile([P, B, N_COPIES * PIXELS], U32, align_bytes=64)
+        x_scales = keep.tile([P, B, N_COPIES * PIXELS], U8, align_bytes=64)
         w_grouped = keep.tile([P, O_TILES, TAPS, P, PACK], BF16, align_bytes=64)
         w_codes = keep.tile([P, O_TILES, TAPS, P], U32, align_bytes=64)
         w_scales = keep.tile([P, O_TILES, TAPS, P], U8, align_bytes=64)
 
         def load_x(b):
-            nc.scalar.dma_start(
+            nc.sync.dma_start(
                 out=x_raw[:, b].rearrange("p t h w -> p t (h w)"),
                 in_=x[b].rearrange("(t p) h w -> p t (h w)", p=P),
             )
@@ -56,23 +54,27 @@ def tile_r8convf_pa_s_kernel(tc, x, weight, out):
                 in_=weight[ot * P : (ot + 1) * P].rearrange("o c k -> o (c k)"),
             )
 
-        def move_x(dx):
-            first, last = max(0, -dx), W - max(0, dx)
-            nc.vector.tensor_copy(
-                out=x_moved[:, dx + 1, 1 : 1 + H, :, first:last, :],
-                in_=x_raw[:, :, :, :, first + dx : last + dx].rearrange("p b t h w -> p h b w t"),
-            )
+        def move_x(b):
+            for dx in (-1, 0, 1):
+                first, last = max(0, -dx), W - max(0, dx)
+                nc.vector.tensor_copy(
+                    out=x_moved[:, b, dx + 1, 1 : 1 + H, first:last, :],
+                    in_=x_raw[:, b, :, :, first + dx : last + dx].rearrange("p t h w -> p h w t"),
+                )
 
-        def quantise_copy(copy, dy, dx):
+        def quantise_copy(b, copy, dy, dx):
+            columns = slice(copy * PIXELS, (copy + 1) * PIXELS)
             nc.vector.quantize_mx(
-                out=x_codes[:, copy].bitcast(FP8X4),
-                scales=x_scales[:, copy],
-                in_=x_moved[:, dx + 1, 1 + dy : 1 + dy + H].rearrange("p h b w t -> p (h b w t)"),
+                out=x_codes[:, b, columns].bitcast(FP8X4),
+                scales=x_scales[:, b, columns],
+                in_=x_moved[:, b, dx + 1, 1 + dy : 1 + dy + H].rearrange("p h w t -> p (h w t)"),
             )
 
-        def quantise_opposite_copies(d):
-            for copy in (d + HALF_TURN, d):
-                quantise_copy(copy, STEPS[copy][0], STEPS[copy][1])
+        def quantise_x(b):
+            for d, (dy, dx) in enumerate(STEPS):
+                quantise_copy(b, d, dy, dx)
+            for copy in range(N_STEPS, N_COPIES):
+                quantise_copy(b, copy, 0, 0)
 
         def transpose_weight(ot):
             for k in range(TAPS):
@@ -89,50 +91,47 @@ def tile_r8convf_pa_s_kernel(tc, x, weight, out):
                     in_=w_grouped[:, ot, k].rearrange("p o t -> p (o t)"),
                 )
 
-        def convolve(ot):
-            for d0 in range(0, N_STEPS, STEPS_PER_STORE):
-                result = stage.tile([P, B, STEPS_PER_STORE, H, W], F32)
-                for i in range(STEPS_PER_STORE):
-                    d = d0 + i
-                    copy_of_tap = ((d + HALF_TURN) % N_STEPS, UNMOVED, d)
-                    acc = psum.tile([P, PIXELS], F32, tag="bank", name="acc")
-                    for k in range(TAPS):
-                        nc.tensor.matmul_mx(
-                            out=acc[:],
-                            lhsT=w_codes[:, ot, k].bitcast(FP8X4),
-                            lhsT_scale=w_scales[:, ot, k],
-                            rhs=x_codes[:, copy_of_tap[k]].bitcast(FP8X4),
-                            rhs_scale=x_scales[:, copy_of_tap[k]],
-                            start=(k == 0),
-                            stop=(k == TAPS - 1),
-                        )
-                    nc.scalar.copy(
-                        out=result[:, :, i], in_=acc[:].rearrange("p (h b w) -> p b h w", h=H, b=B)
+        def convolve(ot, b):
+            for d0 in range(0, N_STEPS, STEPS_PER_BANK):
+                first_copy = {0: (d0 + N_STEPS // 2) % N_STEPS, 1: N_STEPS, 2: d0}
+                acc = psum.tile([P, STEPS_PER_BANK * PIXELS], F32, tag="bank", name="acc")
+                for k in range(TAPS):
+                    columns = slice(first_copy[k] * PIXELS, (first_copy[k] + STEPS_PER_BANK) * PIXELS)
+                    nc.tensor.matmul_mx(
+                        out=acc[:],
+                        lhsT=w_codes[:, ot, k].bitcast(FP8X4),
+                        lhsT_scale=w_scales[:, ot, k],
+                        rhs=x_codes[:, b, columns].bitcast(FP8X4),
+                        rhs_scale=x_scales[:, b, columns],
+                        start=(k == 0),
+                        stop=(k == TAPS - 1),
                     )
+                result = stage.tile([P, STEPS_PER_BANK * PIXELS], F32)
+                nc.scalar.copy(out=result[:], in_=acc[:])
                 nc.sync.dma_start(
-                    out=out[:, ot * P : (ot + 1) * P, d0 : d0 + STEPS_PER_STORE].rearrange(
-                        "b o d h w -> o b (d h w)"
+                    out=out[b, ot * P : (ot + 1) * P, d0 : d0 + STEPS_PER_BANK].rearrange(
+                        "o d h w -> o (d h w)"
                     ),
-                    in_=result[:].rearrange("p b d h w -> p b (d h w)"),
+                    in_=result[:],
                 )
 
-        for b in range(B):
-            load_x(b)
-        for ot in range(O_TILES):
-            load_weight(ot)
+        load_x(0)
+        load_weight(0)
+        load_weight(1)
+        load_x(1)
         make_identity(nc, identity[:])
-        nc.vector.memset(x_moved[:].rearrange("p a h b w t -> p (a h b w t)").bitcast(I32), 0)
+        for b in range(B):
+            nc.vector.memset(x_moved[:, b].rearrange("p a h w t -> p (a h w t)").bitcast(I32), 0)
 
-        for dx in (-1, 0, 1):
-            move_x(dx)
+        move_x(0)
         transpose_weight(0)
-        quantise_copy(UNMOVED, 0, 0)
-        quantise_opposite_copies(0)
-        quantise_opposite_copies(1)
+        quantise_x(0)
         transpose_weight(1)
         quantise_weight(0)
-        quantise_opposite_copies(2)
-        quantise_opposite_copies(3)
+        move_x(1)
         quantise_weight(1)
-        convolve(0)
-        convolve(1)
+        convolve(0, 0)
+        convolve(1, 0)
+        quantise_x(1)
+        convolve(0, 1)
+        convolve(1, 1)

from contextlib import ExitStack

import concourse.mybir as mybir
from concourse.masks import make_identity

BF16 = mybir.dt.bfloat16
F32 = mybir.dt.float32
I32 = mybir.dt.int32
U32 = mybir.dt.uint32
U8 = mybir.dt.uint8
FP8X4 = mybir.dt.float8_e4m3fn_x4

B, C, H, W, O, TAPS = 2, 512, 8, 16, 256, 3
STEPS = ((0, 1), (1, 1), (1, 0), (1, -1), (0, -1), (-1, -1), (-1, 0), (-1, 1))
N_STEPS = len(STEPS)

P = 128
PACK = 4
PIXELS = H * W
O_TILES = O // P
STEPS_PER_BANK = 4
N_COPIES = N_STEPS + STEPS_PER_BANK

FLOPS = 2 * B * H * W * C * O * TAPS


def tile_r8convf_pa_s_kernel(tc, x, weight, out):
    nc = tc.nc
    with ExitStack() as ctx:
        ctx.enter_context(tc.manual_schedule())
        keep = ctx.enter_context(tc.tile_pool(name="keep", bufs=1))
        stage = ctx.enter_context(tc.tile_pool(name="stage", bufs=4))
        psum = ctx.enter_context(tc.psum_pool(name="psum", bufs=8))

        identity = keep.tile([P, P], BF16)
        x_raw = keep.tile([P, B, PACK, H, W], BF16)
        w_raw = keep.tile([P, O_TILES, C, TAPS], BF16)
        x_moved = keep.tile([P, B, 3, H + 2, W, PACK], BF16, align_bytes=64)
        x_codes = keep.tile([P, B, N_COPIES * PIXELS], U32, align_bytes=64)
        x_scales = keep.tile([P, B, N_COPIES * PIXELS], U8, align_bytes=64)
        w_grouped = keep.tile([P, O_TILES, TAPS, P, PACK], BF16, align_bytes=64)
        w_codes = keep.tile([P, O_TILES, TAPS, P], U32, align_bytes=64)
        w_scales = keep.tile([P, O_TILES, TAPS, P], U8, align_bytes=64)

        def load_x(b):
            nc.sync.dma_start(
                out=x_raw[:, b].rearrange("p t h w -> p t (h w)"),
                in_=x[b].rearrange("(t p) h w -> p t (h w)", p=P),
            )

        def load_weight(ot):
            nc.sync.dma_start(
                out=w_raw[:, ot].rearrange("p c k -> p (c k)"),
                in_=weight[ot * P : (ot + 1) * P].rearrange("o c k -> o (c k)"),
            )

        def move_x(b):
            for dx in (-1, 0, 1):
                first, last = max(0, -dx), W - max(0, dx)
                nc.vector.tensor_copy(
                    out=x_moved[:, b, dx + 1, 1 : 1 + H, first:last, :],
                    in_=x_raw[:, b, :, :, first + dx : last + dx].rearrange("p t h w -> p h w t"),
                )

        def quantise_copy(b, copy, dy, dx):
            columns = slice(copy * PIXELS, (copy + 1) * PIXELS)
            nc.vector.quantize_mx(
                out=x_codes[:, b, columns].bitcast(FP8X4),
                scales=x_scales[:, b, columns],
                in_=x_moved[:, b, dx + 1, 1 + dy : 1 + dy + H].rearrange("p h w t -> p (h w t)"),
            )

        def quantise_x(b):
            for d, (dy, dx) in enumerate(STEPS):
                quantise_copy(b, d, dy, dx)
            for copy in range(N_STEPS, N_COPIES):
                quantise_copy(b, copy, 0, 0)

        def transpose_weight(ot):
            for k in range(TAPS):
                w_t = psum.tile([P, PACK, P], BF16, tag="bank", name="w_t")
                for t in range(PACK):
                    nc.tensor.transpose(w_t[:, t, :], w_raw[:, ot, t * P : (t + 1) * P, k], identity[:])
                nc.scalar.copy(out=w_grouped[:, ot, k], in_=w_t[:].rearrange("p t o -> p o t"))

        def quantise_weight(ot):
            for k in range(TAPS):
                nc.vector.quantize_mx(
                    out=w_codes[:, ot, k].bitcast(FP8X4),
                    scales=w_scales[:, ot, k],
                    in_=w_grouped[:, ot, k].rearrange("p o t -> p (o t)"),
                )

        def convolve(ot, b):
            for d0 in range(0, N_STEPS, STEPS_PER_BANK):
                first_copy = {0: (d0 + N_STEPS // 2) % N_STEPS, 1: N_STEPS, 2: d0}
                acc = psum.tile([P, STEPS_PER_BANK * PIXELS], F32, tag="bank", name="acc")
                for k in range(TAPS):
                    columns = slice(first_copy[k] * PIXELS, (first_copy[k] + STEPS_PER_BANK) * PIXELS)
                    nc.tensor.matmul_mx(
                        out=acc[:],
                        lhsT=w_codes[:, ot, k].bitcast(FP8X4),
                        lhsT_scale=w_scales[:, ot, k],
                        rhs=x_codes[:, b, columns].bitcast(FP8X4),
                        rhs_scale=x_scales[:, b, columns],
                        start=(k == 0),
                        stop=(k == TAPS - 1),
                    )
                result = stage.tile([P, STEPS_PER_BANK * PIXELS], F32)
                nc.scalar.copy(out=result[:], in_=acc[:])
                nc.sync.dma_start(
                    out=out[b, ot * P : (ot + 1) * P, d0 : d0 + STEPS_PER_BANK].rearrange(
                        "o d h w -> o (d h w)"
                    ),
                    in_=result[:],
                )

        load_x(0)
        load_weight(0)
        load_weight(1)
        load_x(1)
        make_identity(nc, identity[:])
        for b in range(B):
            nc.vector.memset(x_moved[:, b].rearrange("p a h w t -> p (a h w t)").bitcast(I32), 0)

        move_x(0)
        transpose_weight(0)
        quantise_x(0)
        transpose_weight(1)
        quantise_weight(0)
        move_x(1)
        quantise_weight(1)
        convolve(0, 0)
        convolve(1, 0)
        quantise_x(1)
        convolve(0, 1)
        convolve(1, 1)
